import numpy as np
import ml_dtypes

BF16 = ml_dtypes.bfloat16


def bf(x):
    return np.asarray(x, np.float32).astype(BF16)


def f32(x):
    return np.asarray(x, np.float32)


def f64(x):
    return np.asarray(x).astype(np.float64)


def striped(idx):
    return np.tile(idx.reshape(-1, 16).T, (8, 1))


D, T, S, N = 128, 1024, 1024, 1024
SCALE = 1.0 / np.sqrt(D)
MASK_STD = 1.5
V_STD = 2.0


def setup_inputs():
    return {"mask": f32(MASK_STD * np.random.standard_normal((T, S))), "q": bf(np.random.standard_normal((D, N))), "kc": bf(np.random.standard_normal((D, T))), "vc": bf(V_STD * np.random.standard_normal((T, D))), "offs": striped(np.random.permutation(S)[:N])}


def reference(mask, q, kc, vc, offs):
    idx = offs[:16].T.reshape(-1)
    w = SCALE * (f64(kc).T @ f64(q)) + f64(mask)[:, idx]
    e = np.exp(w)
    p = e / e.sum(axis=0, keepdims=True)
    return f64(vc).T @ p

@@ -1,0 +1,133 @@
+import math
+
+import concourse.mybir as mybir
+from concourse.masks import make_identity
+
+F32 = mybir.dt.float32
+BF16 = mybir.dt.bfloat16
+U16 = mybir.dt.uint16
+ADD = mybir.AluOpType.add
+COPY = mybir.ActivationFunctionType.Copy
+EXP = mybir.ActivationFunctionType.Exp
+
+P = 128
+D, T, S, N = 128, 1024, 1024, 1024
+SCALE = 1.0 / math.sqrt(D)
+KEY_BLOCKS = T // P
+BANK = 512
+PAIR = 2
+CUT = PAIR * P
+CUTS = N // CUT
+PITCH = 160
+AHEAD = 2
+LATE = 2
+FLOPS = 4 * D * T * N
+
+
+def tile_sdpasimple_kernel(tc, mask, q, kc, vc, offs, out):
+    nc = tc.nc
+    with (
+        tc.tile_pool(name="held", bufs=1) as held,
+        tc.tile_pool(name="work", bufs=4) as work,
+        tc.tile_pool(name="small", bufs=8) as small,
+        tc.psum_pool(name="product_banks", bufs=1) as product_banks,
+        tc.psum_pool(name="other_banks", bufs=4) as other_banks,
+    ):
+        offsets = held.tile([P, N // 16], U16, name="offsets")
+        kc_sb = held.tile([D, T], BF16, name="kc_sb")
+        q_sb = held.tile([D, N], BF16, name="q_sb")
+        mask_sb = [held.tile([P, S], F32, name=f"mask{b}") for b in range(KEY_BLOCKS)]
+        vc_ones = held.tile([P, KEY_BLOCKS, PITCH], BF16, name="vc_ones")
+        nc.gpsimd.memset(vc_ones[:, :, D:PITCH], 1.0)
+        zeros = held.tile([P, P], BF16, name="zeros")
+        nc.gpsimd.memset(zeros[:], 0.0)
+        nc.sync.dma_start(offsets[:], offs)
+        nc.scalar.dma_start(kc_sb[:, 0 : AHEAD * P], kc[:, 0 : AHEAD * P])
+        nc.sync.dma_start(q_sb[:, 0:BANK], q[:, 0:BANK])
+        nc.scalar.dma_start(q_sb[:, BANK:N], q[:, BANK:N])
+        nc.sync.dma_start(mask_sb[0][:], mask[0:P, :])
+        nc.sync.dma_start(kc_sb[:, AHEAD * P : T], kc[:, AHEAD * P : T])
+        nc.sync.dma_start(vc_ones[:, :, 0:D], vc.rearrange("(b p) d -> p b d", p=P))
+        for b in range(1, KEY_BLOCKS):
+            nc.sync.dma_start(mask_sb[b][:], mask[b * P : (b + 1) * P, :])
+        identity = held.tile([P, P], F32, name="identity")
+        make_identity(nc, identity[:])
+
+        scaled = {}
+        products = []
+        inverses = {}
+        turned = {}
+
+        def scores(b):
+            scaled_sb = work.tile([P, N], F32, name="scaled_sb")
+            for lo in range(0, N, BANK):
+                score_ps = other_banks.tile([P, BANK], F32, name="score_ps", tag="bank")
+                nc.tensor.matmul(
+                    score_ps[:],
+                    kc_sb[:, b * P : (b + 1) * P],
+                    q_sb[:, lo : lo + BANK],
+                    start=True,
+                    stop=True,
+                )
+                nc.scalar.activation(scaled_sb[:, lo : lo + BANK], score_ps[:], COPY, scale=SCALE)
+            scaled[b] = scaled_sb
+
+        def weights(b, w_sb, e_sb, lo, hi):
+            nc.vector.tensor_tensor(
+                w_sb[:, lo:hi],
+                mask_sb[b][:].indirect(offsets[:, lo // 16 : hi // 16]),
+                scaled[b][:, lo:hi],
+                ADD,
+            )
+            nc.scalar.activation(e_sb[:, lo:hi], w_sb[:, lo:hi], EXP)
+            for c in range(lo // P, hi // P):
+                cut, i = divmod(c, PAIR)
+                nc.tensor.matmul(
+                    products[cut][:, i, :],
+                    e_sb[:, c * P : (c + 1) * P],
+                    vc_ones[:, b, :],
+                    start=False,
+                    stop=(b == KEY_BLOCKS - 1 and i == PAIR - 1),
+                )
+
+        def divide(cut):
+            inverse = small.tile([P, PAIR, 1], F32, name="inverse")
+            nc.vector.reciprocal(inverse[:], products[cut][:, :, D : D + 1])
+            out_ps = other_banks.tile([D, CUT], F32, name="out_ps", tag="bank")
+            for i in range(PAIR):
+                normal = small.tile([P, D], F32, name="normal")
+                nc.scalar.activation(
+                    normal[:], products[cut][:, i, 0:D], COPY, scale=inverse[:, i, :]
+                )
+                nc.tensor.transpose(out_ps[:, i * P : (i + 1) * P], normal[:], identity[:])
+            turned[cut] = out_ps
+
+        def leave(cut):
+            out_sb = small.tile([D, CUT], F32, name="out_sb")
+            nc.vector.tensor_copy(out_sb[:], turned[cut][:])
+            nc.sync.dma_start(out[:, cut * CUT : (cut + 1) * CUT], out_sb[:])
+
+        for b in range(AHEAD):
+            scores(b)
+        for cut in range(CUTS):
+            product = product_banks.tile([P, PAIR, PITCH], F32, name=f"product{cut}")
+            nc.tensor.matmul(product[:], zeros[:], q_sb[:, 0 : PAIR * PITCH], start=True, stop=False)
+            products.append(product)
+        for b in range(KEY_BLOCKS):
+            if b + AHEAD < KEY_BLOCKS:
+                scores(b + AHEAD)
+            w_sb = work.tile([P, N], F32, name="w_sb")
+            e_sb = work.tile([P, N], BF16, name="e_sb")
+            if b == 0:
+                for lo in range(0, N, BANK):
+                    weights(b, w_sb, e_sb, lo, lo + BANK)
+            elif b < KEY_BLOCKS - 1:
+                weights(b, w_sb, e_sb, 0, N)
+            else:
+                for cut in range(CUTS + LATE):
+                    if cut < CUTS:
+                        weights(b, w_sb, e_sb, cut * CUT, (cut + 1) * CUT)
+                    if cut >= LATE:
+                        divide(cut - LATE)
+        for cut in range(CUTS):
+            leave(cut)

@@ -7,6 +7,7 @@ F32 = mybir.dt.float32
 BF16 = mybir.dt.bfloat16
 U16 = mybir.dt.uint16
 ADD = mybir.AluOpType.add
+MULT = mybir.AluOpType.mult
 COPY = mybir.ActivationFunctionType.Copy
 EXP = mybir.ActivationFunctionType.Exp
 
@@ -69,7 +70,10 @@ def tile_sdpasimple_kernel(tc, mask, q, kc, vc, offs, out):
                     start=True,
                     stop=True,
                 )
-                nc.scalar.activation(scaled_sb[:, lo : lo + BANK], score_ps[:], COPY, scale=SCALE)
+                if b == 0 and lo == 0:
+                    nc.vector.tensor_scalar(scaled_sb[:, 0:BANK], score_ps[:], SCALE, None, MULT)
+                else:
+                    nc.scalar.activation(scaled_sb[:, lo : lo + BANK], score_ps[:], COPY, scale=SCALE)
             scaled[b] = scaled_sb
 
         def weights(b, w_sb, e_sb, lo, hi):

import math

import concourse.mybir as mybir
from concourse.masks import make_identity

F32 = mybir.dt.float32
BF16 = mybir.dt.bfloat16
U16 = mybir.dt.uint16
ADD = mybir.AluOpType.add
MULT = mybir.AluOpType.mult
COPY = mybir.ActivationFunctionType.Copy
EXP = mybir.ActivationFunctionType.Exp

P = 128
D, T, S, N = 128, 1024, 1024, 1024
SCALE = 1.0 / math.sqrt(D)
KEY_BLOCKS = T // P
BANK = 512
PAIR = 2
CUT = PAIR * P
CUTS = N // CUT
PITCH = 160
AHEAD = 2
LATE = 2
FLOPS = 4 * D * T * N


def tile_sdpasimple_kernel(tc, mask, q, kc, vc, offs, out):
    nc = tc.nc
    with (
        tc.tile_pool(name="held", bufs=1) as held,
        tc.tile_pool(name="work", bufs=4) as work,
        tc.tile_pool(name="small", bufs=8) as small,
        tc.psum_pool(name="product_banks", bufs=1) as product_banks,
        tc.psum_pool(name="other_banks", bufs=4) as other_banks,
    ):
        offsets = held.tile([P, N // 16], U16, name="offsets")
        kc_sb = held.tile([D, T], BF16, name="kc_sb")
        q_sb = held.tile([D, N], BF16, name="q_sb")
        mask_sb = [held.tile([P, S], F32, name=f"mask{b}") for b in range(KEY_BLOCKS)]
        vc_ones = held.tile([P, KEY_BLOCKS, PITCH], BF16, name="vc_ones")
        nc.gpsimd.memset(vc_ones[:, :, D:PITCH], 1.0)
        zeros = held.tile([P, P], BF16, name="zeros")
        nc.gpsimd.memset(zeros[:], 0.0)
        nc.sync.dma_start(offsets[:], offs)
        nc.scalar.dma_start(kc_sb[:, 0 : AHEAD * P], kc[:, 0 : AHEAD * P])
        nc.sync.dma_start(q_sb[:, 0:BANK], q[:, 0:BANK])
        nc.scalar.dma_start(q_sb[:, BANK:N], q[:, BANK:N])
        nc.sync.dma_start(mask_sb[0][:], mask[0:P, :])
        nc.sync.dma_start(kc_sb[:, AHEAD * P : T], kc[:, AHEAD * P : T])
        nc.sync.dma_start(vc_ones[:, :, 0:D], vc.rearrange("(b p) d -> p b d", p=P))
        for b in range(1, KEY_BLOCKS):
            nc.sync.dma_start(mask_sb[b][:], mask[b * P : (b + 1) * P, :])
        identity = held.tile([P, P], F32, name="identity")
        make_identity(nc, identity[:])

        scaled = {}
        products = []
        inverses = {}
        turned = {}

        def scores(b):
            scaled_sb = work.tile([P, N], F32, name="scaled_sb")
            for lo in range(0, N, BANK):
                score_ps = other_banks.tile([P, BANK], F32, name="score_ps", tag="bank")
                nc.tensor.matmul(
                    score_ps[:],
                    kc_sb[:, b * P : (b + 1) * P],
                    q_sb[:, lo : lo + BANK],
                    start=True,
                    stop=True,
                )
                if b == 0 and lo == 0:
                    nc.vector.tensor_scalar(scaled_sb[:, 0:BANK], score_ps[:], SCALE, None, MULT)
                else:
                    nc.scalar.activation(scaled_sb[:, lo : lo + BANK], score_ps[:], COPY, scale=SCALE)
            scaled[b] = scaled_sb

        def weights(b, w_sb, e_sb, lo, hi):
            nc.vector.tensor_tensor(
                w_sb[:, lo:hi],
                mask_sb[b][:].indirect(offsets[:, lo // 16 : hi // 16]),
                scaled[b][:, lo:hi],
                ADD,
            )
            nc.scalar.activation(e_sb[:, lo:hi], w_sb[:, lo:hi], EXP)
            for c in range(lo // P, hi // P):
                cut, i = divmod(c, PAIR)
                nc.tensor.matmul(
                    products[cut][:, i, :],
                    e_sb[:, c * P : (c + 1) * P],
                    vc_ones[:, b, :],
                    start=False,
                    stop=(b == KEY_BLOCKS - 1 and i == PAIR - 1),
                )

        def divide(cut):
            inverse = small.tile([P, PAIR, 1], F32, name="inverse")
            nc.vector.reciprocal(inverse[:], products[cut][:, :, D : D + 1])
            out_ps = other_banks.tile([D, CUT], F32, name="out_ps", tag="bank")
            for i in range(PAIR):
                normal = small.tile([P, D], F32, name="normal")
                nc.scalar.activation(
                    normal[:], products[cut][:, i, 0:D], COPY, scale=inverse[:, i, :]
                )
                nc.tensor.transpose(out_ps[:, i * P : (i + 1) * P], normal[:], identity[:])
            turned[cut] = out_ps

        def leave(cut):
            out_sb = small.tile([D, CUT], F32, name="out_sb")
            nc.vector.tensor_copy(out_sb[:], turned[cut][:])
            nc.sync.dma_start(out[:, cut * CUT : (cut + 1) * CUT], out_sb[:])

        for b in range(AHEAD):
            scores(b)
        for cut in range(CUTS):
            product = product_banks.tile([P, PAIR, PITCH], F32, name=f"product{cut}")
            nc.tensor.matmul(product[:], zeros[:], q_sb[:, 0 : PAIR * PITCH], start=True, stop=False)
            products.append(product)
        for b in range(KEY_BLOCKS):
            if b + AHEAD < KEY_BLOCKS:
                scores(b + AHEAD)
            w_sb = work.tile([P, N], F32, name="w_sb")
            e_sb = work.tile([P, N], BF16, name="e_sb")
            if b == 0:
                for lo in range(0, N, BANK):
                    weights(b, w_sb, e_sb, lo, lo + BANK)
            elif b < KEY_BLOCKS - 1:
                weights(b, w_sb, e_sb, 0, N)
            else:
                for cut in range(CUTS + LATE):
                    if cut < CUTS:
                        weights(b, w_sb, e_sb, cut * CUT, (cut + 1) * CUT)
                    if cut >= LATE:
                        divide(cut - LATE)
        for cut in range(CUTS):
            leave(cut)
